import numpy as np
import ml_dtypes

BF16 = ml_dtypes.bfloat16


def bf(x):
    return np.asarray(x, np.float32).astype(BF16)


def f32(x):
    return np.asarray(x, np.float32)


def f64(x):
    return np.asarray(x).astype(np.float64)


def striped(idx):
    return np.tile(idx.reshape(-1, 16).T, (8, 1))


C, S, N = 256, 4096, 2048


def setup_inputs():
    return {"obs_emb": f32(np.random.standard_normal((C, S))), "act_x": f32(np.random.standard_normal((C, N))), "type_act": f32(np.random.standard_normal((C, 1))), "type_obs": f32(np.random.standard_normal((C, 1))), "offs": striped(np.random.permutation(np.tile(np.arange(S), 2))[:N])}


def reference(obs_emb, act_x, type_act, type_obs, offs):
    idx = offs[:16].T.reshape(-1)
    other = f64(act_x) + f64(type_act) + f64(type_obs)
    return f64(obs_emb)[:, idx] + other

@@ -1,0 +1,41 @@
+import concourse.mybir as mybir
+
+F32 = mybir.dt.float32
+U16 = mybir.dt.uint16
+ADD = mybir.AluOpType.add
+IDENTITY = mybir.ActivationFunctionType.Identity
+
+P = 128
+C, S, N = 256, 4096, 2048
+BLOCKS = C // P
+
+
+def tile_transformerrope_kernel(tc, obs_emb, act_x, type_act, type_obs, offs, out):
+    nc = tc.nc
+    with (
+        tc.tile_pool(name="held", bufs=1) as held,
+        tc.tile_pool(name="block", bufs=BLOCKS) as block,
+    ):
+        offsets = held.tile([P, N // 16], U16, name="offsets")
+        nc.sync.dma_start(offsets[:], offs)
+
+        for b in range(BLOCKS):
+            rows = slice(b * P, (b + 1) * P)
+
+            table = block.tile([P, S], F32)
+            nc.sync.dma_start(table[:], obs_emb[rows, :])
+            action = block.tile([P, N], F32)
+            nc.sync.dma_start(action[:], act_x[rows, :])
+            bias_act = block.tile([P, 1], F32)
+            nc.scalar.dma_start(bias_act[:], type_act[rows, :])
+            bias_obs = block.tile([P, 1], F32)
+            nc.scalar.dma_start(bias_obs[:], type_obs[rows, :])
+
+            bias = block.tile([P, 1], F32)
+            nc.vector.tensor_tensor(bias[:], bias_act[:], bias_obs[:], ADD)
+            other = block.tile([P, N], F32)
+            nc.scalar.activation(other[:], action[:], IDENTITY, bias=bias[:], scale=1.0)
+
+            result = block.tile([P, N], F32)
+            nc.vector.tensor_tensor(result[:], table[:].indirect(offsets[:]), other[:], ADD)
+            nc.sync.dma_start(out[rows, :], result[:])

@@ -8,6 +8,8 @@ IDENTITY = mybir.ActivationFunctionType.Identity
 P = 128
 C, S, N = 256, 4096, 2048
 BLOCKS = C // P
+PIECE = 512
+PIECES = N // PIECE
 
 
 def tile_transformerrope_kernel(tc, obs_emb, act_x, type_act, type_obs, offs, out):
@@ -19,23 +21,38 @@ def tile_transformerrope_kernel(tc, obs_emb, act_x, type_act, type_obs, offs, ou
         offsets = held.tile([P, N // 16], U16, name="offsets")
         nc.sync.dma_start(offsets[:], offs)
 
+        tables, actions, biases = [], [], []
         for b in range(BLOCKS):
             rows = slice(b * P, (b + 1) * P)
 
-            table = block.tile([P, S], F32)
-            nc.sync.dma_start(table[:], obs_emb[rows, :])
-            action = block.tile([P, N], F32)
-            nc.sync.dma_start(action[:], act_x[rows, :])
             bias_act = block.tile([P, 1], F32)
             nc.scalar.dma_start(bias_act[:], type_act[rows, :])
             bias_obs = block.tile([P, 1], F32)
             nc.scalar.dma_start(bias_obs[:], type_obs[rows, :])
-
             bias = block.tile([P, 1], F32)
-            nc.vector.tensor_tensor(bias[:], bias_act[:], bias_obs[:], ADD)
-            other = block.tile([P, N], F32)
-            nc.scalar.activation(other[:], action[:], IDENTITY, bias=bias[:], scale=1.0)
+            nc.scalar.activation(bias[:], bias_act[:], IDENTITY, bias=bias_obs[:], scale=1.0)
 
+            table = block.tile([P, S], F32)
+            action = block.tile([P, N], F32)
+            nc.sync.dma_start(action[:, 0:PIECE], act_x[rows, 0:PIECE])
+            nc.sync.dma_start(table[:], obs_emb[rows, :])
+            for i in range(1, PIECES):
+                steps = slice(i * PIECE, (i + 1) * PIECE)
+                nc.sync.dma_start(action[:, steps], act_x[rows, steps])
+
+            tables.append(table)
+            actions.append(action)
+            biases.append(bias)
+
+        for b in range(BLOCKS):
+            rows = slice(b * P, (b + 1) * P)
+            other = block.tile([P, N], F32)
             result = block.tile([P, N], F32)
-            nc.vector.tensor_tensor(result[:], table[:].indirect(offsets[:]), other[:], ADD)
-            nc.sync.dma_start(out[rows, :], result[:])
+            for i in range(PIECES):
+                steps = slice(i * PIECE, (i + 1) * PIECE)
+                nc.scalar.activation(
+                    other[:, steps], actions[b][:, steps], IDENTITY, bias=biases[b][:], scale=1.0
+                )
+                looked_up = tables[b][:].indirect(offsets[:, i * PIECE // 16 : (i + 1) * PIECE // 16])
+                nc.vector.tensor_tensor(result[:, steps], looked_up, other[:, steps], ADD)
+                nc.sync.dma_start(out[rows, steps], result[:, steps])

@@ -30,7 +30,7 @@ def tile_transformerrope_kernel(tc, obs_emb, act_x, type_act, type_obs, offs, ou
             bias_obs = block.tile([P, 1], F32)
             nc.scalar.dma_start(bias_obs[:], type_obs[rows, :])
             bias = block.tile([P, 1], F32)
-            nc.scalar.activation(bias[:], bias_act[:], IDENTITY, bias=bias_obs[:], scale=1.0)
+            nc.vector.tensor_tensor(bias[:], bias_act[:], bias_obs[:], ADD)
 
             table = block.tile([P, S], F32)
             action = block.tile([P, N], F32)

@@ -55,4 +55,7 @@ def tile_transformerrope_kernel(tc, obs_emb, act_x, type_act, type_obs, offs, ou
                 )
                 looked_up = tables[b][:].indirect(offsets[:, i * PIECE // 16 : (i + 1) * PIECE // 16])
                 nc.vector.tensor_tensor(result[:, steps], looked_up, other[:, steps], ADD)
-                nc.sync.dma_start(out[rows, steps], result[:, steps])
+                if b == BLOCKS - 1:
+                    nc.sync.dma_start(out[rows, steps], result[:, steps])
+            if b < BLOCKS - 1:
+                nc.sync.dma_start(out[rows, :], result[:])

@@ -17,20 +17,25 @@ def tile_transformerrope_kernel(tc, obs_emb, act_x, type_act, type_obs, offs, ou
     with (
         tc.tile_pool(name="held", bufs=1) as held,
         tc.tile_pool(name="block", bufs=BLOCKS) as block,
+        tc.psum_pool(name="psum", bufs=BLOCKS) as psum,
     ):
         offsets = held.tile([P, N // 16], U16, name="offsets")
         nc.sync.dma_start(offsets[:], offs)
+
+        type_rows = held.tile([2, C], F32, name="type_rows")
+        nc.scalar.dma_start(type_rows[0:1, :], type_act.rearrange("c one -> one c"))
+        nc.scalar.dma_start(type_rows[1:2, :], type_obs.rearrange("c one -> one c"))
+        ones = held.tile([2, 1], F32, name="ones")
+        nc.vector.memset(ones[:], 1.0)
 
         tables, actions, biases = [], [], []
         for b in range(BLOCKS):
             rows = slice(b * P, (b + 1) * P)
 
-            bias_act = block.tile([P, 1], F32)
-            nc.scalar.dma_start(bias_act[:], type_act[rows, :])
-            bias_obs = block.tile([P, 1], F32)
-            nc.scalar.dma_start(bias_obs[:], type_obs[rows, :])
+            bias_sum = psum.tile([P, 1], F32)
+            nc.tensor.matmul(bias_sum[:], type_rows[:, rows], ones[:])
             bias = block.tile([P, 1], F32)
-            nc.vector.tensor_tensor(bias[:], bias_act[:], bias_obs[:], ADD)
+            nc.vector.tensor_copy(bias[:], bias_sum[:])
 
             table = block.tile([P, S], F32)
             action = block.tile([P, N], F32)
@@ -55,7 +60,4 @@ def tile_transformerrope_kernel(tc, obs_emb, act_x, type_act, type_obs, offs, ou
                 )
                 looked_up = tables[b][:].indirect(offsets[:, i * PIECE // 16 : (i + 1) * PIECE // 16])
                 nc.vector.tensor_tensor(result[:, steps], looked_up, other[:, steps], ADD)
-                if b == BLOCKS - 1:
-                    nc.sync.dma_start(out[rows, steps], result[:, steps])
-            if b < BLOCKS - 1:
-                nc.sync.dma_start(out[rows, :], result[:])
+                nc.sync.dma_start(out[rows, steps], result[:, steps])

@@ -8,8 +8,16 @@ IDENTITY = mybir.ActivationFunctionType.Identity
 P = 128
 C, S, N = 256, 4096, 2048
 BLOCKS = C // P
-PIECE = 512
-PIECES = N // PIECE
+PIECES = ((1024, 1024), (384, 256, 512, 512, 256, 128))
+
+
+def cut(widths):
+    slices, start = [], 0
+    for width in widths:
+        slices.append(slice(start, start + width))
+        start += width
+    assert start == N
+    return slices
 
 
 def tile_transformerrope_kernel(tc, obs_emb, act_x, type_act, type_obs, offs, out):
@@ -31,6 +39,7 @@ def tile_transformerrope_kernel(tc, obs_emb, act_x, type_act, type_obs, offs, ou
         tables, actions, biases = [], [], []
         for b in range(BLOCKS):
             rows = slice(b * P, (b + 1) * P)
+            pieces = cut(PIECES[b])
 
             bias_sum = psum.tile([P, 1], F32)
             nc.tensor.matmul(bias_sum[:], type_rows[:, rows], ones[:])
@@ -39,10 +48,9 @@ def tile_transformerrope_kernel(tc, obs_emb, act_x, type_act, type_obs, offs, ou
 
             table = block.tile([P, S], F32)
             action = block.tile([P, N], F32)
-            nc.sync.dma_start(action[:, 0:PIECE], act_x[rows, 0:PIECE])
+            nc.sync.dma_start(action[:, pieces[0]], act_x[rows, pieces[0]])
             nc.sync.dma_start(table[:], obs_emb[rows, :])
-            for i in range(1, PIECES):
-                steps = slice(i * PIECE, (i + 1) * PIECE)
+            for steps in pieces[1:]:
                 nc.sync.dma_start(action[:, steps], act_x[rows, steps])
 
             tables.append(table)
@@ -53,11 +61,10 @@ def tile_transformerrope_kernel(tc, obs_emb, act_x, type_act, type_obs, offs, ou
             rows = slice(b * P, (b + 1) * P)
             other = block.tile([P, N], F32)
             result = block.tile([P, N], F32)
-            for i in range(PIECES):
-                steps = slice(i * PIECE, (i + 1) * PIECE)
+            for steps in cut(PIECES[b]):
                 nc.scalar.activation(
                     other[:, steps], actions[b][:, steps], IDENTITY, bias=biases[b][:], scale=1.0
                 )
-                looked_up = tables[b][:].indirect(offsets[:, i * PIECE // 16 : (i + 1) * PIECE // 16])
+                looked_up = tables[b][:].indirect(offsets[:, steps.start // 16 : steps.stop // 16])
                 nc.vector.tensor_tensor(result[:, steps], looked_up, other[:, steps], ADD)
                 nc.sync.dma_start(out[rows, steps], result[:, steps])

@@ -8,6 +8,7 @@ IDENTITY = mybir.ActivationFunctionType.Identity
 P = 128
 C, S, N = 256, 4096, 2048
 BLOCKS = C // P
+ALIGN = 256
 PIECES = ((1024, 1024), (384, 256, 512, 512, 256, 128))
 
 
@@ -46,8 +47,8 @@ def tile_transformerrope_kernel(tc, obs_emb, act_x, type_act, type_obs, offs, ou
             bias = block.tile([P, 1], F32)
             nc.vector.tensor_copy(bias[:], bias_sum[:])
 
-            table = block.tile([P, S], F32)
-            action = block.tile([P, N], F32)
+            table = block.tile([P, S], F32, align_bytes=ALIGN)
+            action = block.tile([P, N], F32, align_bytes=ALIGN)
             nc.sync.dma_start(action[:, pieces[0]], act_x[rows, pieces[0]])
             nc.sync.dma_start(table[:], obs_emb[rows, :])
             for steps in pieces[1:]:
@@ -60,7 +61,7 @@ def tile_transformerrope_kernel(tc, obs_emb, act_x, type_act, type_obs, offs, ou
         for b in range(BLOCKS):
             rows = slice(b * P, (b + 1) * P)
             other = block.tile([P, N], F32)
-            result = block.tile([P, N], F32)
+            result = block.tile([P, N], F32, align_bytes=ALIGN)
             for steps in cut(PIECES[b]):
                 nc.scalar.activation(
                     other[:, steps], actions[b][:, steps], IDENTITY, bias=biases[b][:], scale=1.0

@@ -50,7 +50,8 @@ def tile_transformerrope_kernel(tc, obs_emb, act_x, type_act, type_obs, offs, ou
             table = block.tile([P, S], F32, align_bytes=ALIGN)
             action = block.tile([P, N], F32, align_bytes=ALIGN)
             nc.sync.dma_start(action[:, pieces[0]], act_x[rows, pieces[0]])
-            nc.sync.dma_start(table[:], obs_emb[rows, :])
+            for half in (slice(0, S // 2), slice(S // 2, S)):
+                nc.sync.dma_start(table[:, half], obs_emb[rows, half])
             for steps in pieces[1:]:
                 nc.sync.dma_start(action[:, steps], act_x[rows, steps])
 

@@ -29,7 +29,6 @@ def tile_transformerrope_kernel(tc, obs_emb, act_x, type_act, type_obs, offs, ou
         tc.psum_pool(name="psum", bufs=BLOCKS) as psum,
     ):
         offsets = held.tile([P, N // 16], U16, name="offsets")
-        nc.sync.dma_start(offsets[:], offs)
 
         type_rows = held.tile([2, C], F32, name="type_rows")
         nc.scalar.dma_start(type_rows[0:1, :], type_act.rearrange("c one -> one c"))
@@ -50,6 +49,8 @@ def tile_transformerrope_kernel(tc, obs_emb, act_x, type_act, type_obs, offs, ou
             table = block.tile([P, S], F32, align_bytes=ALIGN)
             action = block.tile([P, N], F32, align_bytes=ALIGN)
             nc.sync.dma_start(action[:, pieces[0]], act_x[rows, pieces[0]])
+            if b == 0:
+                nc.sync.dma_start(offsets[:], offs)
             for half in (slice(0, S // 2), slice(S // 2, S)):
                 nc.sync.dma_start(table[:, half], obs_emb[rows, half])
             for steps in pieces[1:]:

@@ -9,16 +9,22 @@ P = 128
 C, S, N = 256, 4096, 2048
 BLOCKS = C // P
 ALIGN = 256
-PIECES = ((1024, 1024), (384, 256, 512, 512, 256, 128))
+PIECES = (
+    ((1024,), (1024,)),
+    ((384,), (192, 192), (384, 384), (384,), (128,)),
+)
 
 
-def cut(widths):
-    slices, start = [], 0
-    for width in widths:
-        slices.append(slice(start, start + width))
-        start += width
-    assert start == N
-    return slices
+def cut(pieces):
+    look_ups, stop = [], 0
+    for widths in pieces:
+        start, loads = stop, []
+        for width in widths:
+            loads.append(slice(stop, stop + width))
+            stop += width
+        look_ups.append((slice(start, stop), loads))
+    assert stop == N
+    return look_ups
 
 
 def tile_transformerrope_kernel(tc, obs_emb, act_x, type_act, type_obs, offs, out):
@@ -39,7 +45,7 @@ def tile_transformerrope_kernel(tc, obs_emb, act_x, type_act, type_obs, offs, ou
         tables, actions, biases = [], [], []
         for b in range(BLOCKS):
             rows = slice(b * P, (b + 1) * P)
-            pieces = cut(PIECES[b])
+            loads = [load for steps, parts in cut(PIECES[b]) for load in parts]
 
             bias_sum = psum.tile([P, 1], F32)
             nc.tensor.matmul(bias_sum[:], type_rows[:, rows], ones[:])
@@ -48,13 +54,13 @@ def tile_transformerrope_kernel(tc, obs_emb, act_x, type_act, type_obs, offs, ou
 
             table = block.tile([P, S], F32, align_bytes=ALIGN)
             action = block.tile([P, N], F32, align_bytes=ALIGN)
-            nc.sync.dma_start(action[:, pieces[0]], act_x[rows, pieces[0]])
+            nc.sync.dma_start(action[:, loads[0]], act_x[rows, loads[0]])
             if b == 0:
                 nc.sync.dma_start(offsets[:], offs)
             for half in (slice(0, S // 2), slice(S // 2, S)):
                 nc.sync.dma_start(table[:, half], obs_emb[rows, half])
-            for steps in pieces[1:]:
-                nc.sync.dma_start(action[:, steps], act_x[rows, steps])
+            for load in loads[1:]:
+                nc.sync.dma_start(action[:, load], act_x[rows, load])
 
             tables.append(table)
             actions.append(action)
@@ -64,10 +70,11 @@ def tile_transformerrope_kernel(tc, obs_emb, act_x, type_act, type_obs, offs, ou
             rows = slice(b * P, (b + 1) * P)
             other = block.tile([P, N], F32)
             result = block.tile([P, N], F32, align_bytes=ALIGN)
-            for steps in cut(PIECES[b]):
-                nc.scalar.activation(
-                    other[:, steps], actions[b][:, steps], IDENTITY, bias=biases[b][:], scale=1.0
-                )
+            for steps, parts in cut(PIECES[b]):
+                for part in parts:
+                    nc.scalar.activation(
+                        other[:, part], actions[b][:, part], IDENTITY, bias=biases[b][:], scale=1.0
+                    )
                 looked_up = tables[b][:].indirect(offsets[:, steps.start // 16 : steps.stop // 16])
                 nc.vector.tensor_tensor(result[:, steps], looked_up, other[:, steps], ADD)
                 nc.sync.dma_start(out[rows, steps], result[:, steps])

@@ -11,7 +11,7 @@ BLOCKS = C // P
 ALIGN = 256
 PIECES = (
     ((1024,), (1024,)),
-    ((384,), (192, 192), (384, 384), (384,), (128,)),
+    ((384,), (192,), (288, 288), (512,), (256,), (128,)),
 )
 
 

@@ -11,7 +11,7 @@ BLOCKS = C // P
 ALIGN = 256
 PIECES = (
     ((1024,), (1024,)),
-    ((384,), (192,), (288, 288), (512,), (256,), (128,)),
+    ((384,), (192,), (192, 192, 192), (256, 256), (256,), (128,)),
 )
 
 
@@ -57,8 +57,7 @@ def tile_transformerrope_kernel(tc, obs_emb, act_x, type_act, type_obs, offs, ou
             nc.sync.dma_start(action[:, loads[0]], act_x[rows, loads[0]])
             if b == 0:
                 nc.sync.dma_start(offsets[:], offs)
-            for half in (slice(0, S // 2), slice(S // 2, S)):
-                nc.sync.dma_start(table[:, half], obs_emb[rows, half])
+            nc.sync.dma_start(table[:], obs_emb[rows, :])
             for load in loads[1:]:
                 nc.sync.dma_start(action[:, load], act_x[rows, load])
 

import concourse.mybir as mybir

F32 = mybir.dt.float32
U16 = mybir.dt.uint16
ADD = mybir.AluOpType.add
IDENTITY = mybir.ActivationFunctionType.Identity

P = 128
C, S, N = 256, 4096, 2048
BLOCKS = C // P
ALIGN = 256
PIECES = (
    ((1024,), (1024,)),
    ((384,), (192,), (192, 192, 192), (256, 256), (256,), (128,)),
)


def cut(pieces):
    look_ups, stop = [], 0
    for widths in pieces:
        start, loads = stop, []
        for width in widths:
            loads.append(slice(stop, stop + width))
            stop += width
        look_ups.append((slice(start, stop), loads))
    assert stop == N
    return look_ups


def tile_transformerrope_kernel(tc, obs_emb, act_x, type_act, type_obs, offs, out):
    nc = tc.nc
    with (
        tc.tile_pool(name="held", bufs=1) as held,
        tc.tile_pool(name="block", bufs=BLOCKS) as block,
        tc.psum_pool(name="psum", bufs=BLOCKS) as psum,
    ):
        offsets = held.tile([P, N // 16], U16, name="offsets")

        type_rows = held.tile([2, C], F32, name="type_rows")
        nc.scalar.dma_start(type_rows[0:1, :], type_act.rearrange("c one -> one c"))
        nc.scalar.dma_start(type_rows[1:2, :], type_obs.rearrange("c one -> one c"))
        ones = held.tile([2, 1], F32, name="ones")
        nc.vector.memset(ones[:], 1.0)

        tables, actions, biases = [], [], []
        for b in range(BLOCKS):
            rows = slice(b * P, (b + 1) * P)
            loads = [load for steps, parts in cut(PIECES[b]) for load in parts]

            bias_sum = psum.tile([P, 1], F32)
            nc.tensor.matmul(bias_sum[:], type_rows[:, rows], ones[:])
            bias = block.tile([P, 1], F32)
            nc.vector.tensor_copy(bias[:], bias_sum[:])

            table = block.tile([P, S], F32, align_bytes=ALIGN)
            action = block.tile([P, N], F32, align_bytes=ALIGN)
            nc.sync.dma_start(action[:, loads[0]], act_x[rows, loads[0]])
            if b == 0:
                nc.sync.dma_start(offsets[:], offs)
            nc.sync.dma_start(table[:], obs_emb[rows, :])
            for load in loads[1:]:
                nc.sync.dma_start(action[:, load], act_x[rows, load])

            tables.append(table)
            actions.append(action)
            biases.append(bias)

        for b in range(BLOCKS):
            rows = slice(b * P, (b + 1) * P)
            other = block.tile([P, N], F32)
            result = block.tile([P, N], F32, align_bytes=ALIGN)
            for steps, parts in cut(PIECES[b]):
                for part in parts:
                    nc.scalar.activation(
                        other[:, part], actions[b][:, part], IDENTITY, bias=biases[b][:], scale=1.0
                    )
                looked_up = tables[b][:].indirect(offsets[:, steps.start // 16 : steps.stop // 16])
                nc.vector.tensor_tensor(result[:, steps], looked_up, other[:, steps], ADD)
                nc.sync.dma_start(out[rows, steps], result[:, steps])
